import numpy as np
import ml_dtypes


def mxq(x, axis, fmt="e4m3"):
    dtype, down = {"e4m3": (ml_dtypes.float8_e4m3fn, 7), "e5m2": (ml_dtypes.float8_e5m2, 14)}[fmt]
    v = np.moveaxis(np.asarray(x, np.float32).astype(ml_dtypes.bfloat16).astype(np.float64), axis, -1)
    blocks = v.reshape(v.shape[:-1] + (-1, 32))
    amax = np.abs(blocks).max(-1, keepdims=True)
    byte = np.maximum(np.where(amax > 0, np.frexp(amax)[1] - 1 + 127, 0) - down, 1)
    scale = np.exp2(byte - 127.0)
    codes = (blocks / scale).astype(np.float32).astype(dtype).astype(np.float64)
    return np.moveaxis((codes * scale).reshape(v.shape), -1, axis)


WIDE = False


def mx_kscale(k):
    if not WIDE:
        return np.ones(k)
    levels = np.array([10, -10, 5, -5, 0])
    if k % 512:
        return np.exp2(np.random.permutation(np.resize(levels, k // 32))).repeat(32)
    a = np.empty((k // 512, 16))
    for p in range(k // 512):
        a[p, :8] = np.random.permutation(np.resize(levels, 8))
        for g in range(8):
            far = levels[np.abs(levels - a[p, g]) >= 10]
            a[p, g + 8] = far[np.random.randint(len(far))]
    return np.exp2(a.ravel()).repeat(32)


BF16 = ml_dtypes.bfloat16


def bf(x):
    return np.asarray(x, np.float32).astype(BF16)


def f64(x):
    return np.asarray(x).astype(np.float64)


N, P, D, E, F = 1024, 3, 512, 1024, 1024


def setup_inputs():
    s = mx_kscale(D)
    x = np.random.standard_normal((N, P, D)) + 0.5 * np.random.standard_normal((1, P, D))
    return {"x": bf(x * s),
            "w1a": bf(np.random.standard_normal((D, E)) / np.sqrt(D) / s[:, None]),
            "w2a": bf(np.random.standard_normal((D, E)) / np.sqrt(D) / s[:, None])}


def reference(x, w1a, w2a):
    h = f64(x)
    neigh = (h.sum(axis=1, keepdims=True) - h) * 0.5
    return (mxq(h, 2, "e4m3") @ mxq(f64(w2a), 0, "e4m3")) + (mxq(neigh, 2, "e4m3") @ mxq(f64(w1a), 0, "e4m3"))

@@ -1,0 +1,218 @@
+from contextlib import ExitStack
+
+import concourse.mybir as mybir
+from concourse.masks import make_identity
+
+F32 = mybir.dt.float32
+BF16 = mybir.dt.bfloat16
+U32 = mybir.dt.uint32
+U8 = mybir.dt.uint8
+FP8X4 = mybir.dt.float8_e4m3fn_x4
+ADD = mybir.AluOpType.add
+MULT = mybir.AluOpType.mult
+
+P = 128
+PACK = 4
+ITEMS, HOPS, K, E = 1024, 3, 512, 1024
+WORDS = K // 2
+TILES = ITEMS // P
+N_PASS = 512
+HALVES = E // N_PASS
+W_CHUNK = 256
+RUN = 4
+AHEAD = 2
+
+FLOPS = 2 * 2 * ITEMS * HOPS * K * E
+
+
+def load_weight(nc, raw, w):
+    nc.sync.dma_start(out=raw[:], in_=w.rearrange("(q t) c -> q t c", t=PACK))
+
+
+def regroup_weight(nc, raw, grouped, c):
+    for copy, first in ((nc.vector.tensor_copy, c * N_PASS), (nc.scalar.copy, c * N_PASS + W_CHUNK)):
+        cols = slice(first, first + W_CHUNK)
+        copy(
+            out=grouped[:, cols, :].rearrange("q (c i) t -> q c t i", i=RUN),
+            in_=raw[:, :, cols].rearrange("q t (c i) -> q c t i", i=RUN),
+        )
+
+
+def quantise_weight(nc, grouped, codes, scales, c):
+    cols = slice(c * N_PASS, (c + 1) * N_PASS)
+    nc.vector.quantize_mx(
+        out=codes[:, cols].bitcast(FP8X4),
+        scales=scales[:, cols],
+        in_=grouped[:, cols, :].rearrange("q c t -> q (c t)"),
+    )
+
+
+def tile_dogtaitujuanji_pa_kernel(tc, x, w1a, w2a, out):
+    nc = tc.nc
+    with ExitStack() as ctx:
+        keep = ctx.enter_context(tc.tile_pool(name="keep", bufs=1))
+        rows = ctx.enter_context(tc.tile_pool(name="rows", bufs=TILES))
+        turns = ctx.enter_context(tc.tile_pool(name="turns", bufs=AHEAD + 1))
+        work = ctx.enter_context(tc.tile_pool(name="work", bufs=2))
+        operands = ctx.enter_context(tc.tile_pool(name="operands", bufs=AHEAD + 2))
+        results = ctx.enter_context(tc.tile_pool(name="results", bufs=6))
+        flipped = ctx.enter_context(tc.psum_pool(name="flipped", bufs=HOPS))
+        sums = ctx.enter_context(tc.psum_pool(name="sums", bufs=8 - HOPS))
+        ctx.enter_context(tc.manual_schedule())
+
+        w2a_raw = keep.tile([P, PACK, E], BF16)
+        w1a_raw = keep.tile([P, PACK, E], BF16)
+        x_rows = []
+        for i in range(TILES):
+            x_tile = rows.tile([P, HOPS * K], BF16, name="x_tile")
+            x_rows.append(x_tile)
+
+        def load_x(i, first_hop, hops):
+            nc.sync.dma_start(
+                out=x_rows[i][:, first_hop * K : (first_hop + hops) * K],
+                in_=x[i * P : (i + 1) * P, first_hop : first_hop + hops, :].rearrange(
+                    "n p k -> n (p k)"
+                ),
+            )
+
+        for p in range(HOPS):
+            load_x(0, p, 1)
+        load_weight(nc, w2a_raw, w2a)
+        load_x(1, 0, HOPS)
+        load_weight(nc, w1a_raw, w1a)
+        for i in range(2, TILES):
+            load_x(i, 0, HOPS)
+
+        identity = keep.tile([P, P], F32)
+        make_identity(nc, identity[:])
+
+        w2a_grouped = keep.tile([P, E, PACK], BF16, align_bytes=64)
+        w1a_grouped = keep.tile([P, E, PACK], BF16, align_bytes=64)
+        w2a_codes = keep.tile([P, E], U32, align_bytes=64)
+        w1a_codes = keep.tile([P, E], U32, align_bytes=64)
+        w2a_scales = keep.tile([P, E], U8, align_bytes=64)
+        w1a_scales = keep.tile([P, E], U8, align_bytes=64)
+
+        width = P * PACK
+        turned = {}
+        prepared = {}
+
+        def turn(i, copy_out):
+            x_words = x_rows[i][:].bitcast(F32)
+            x_t = turns.tile([P, HOPS * width], BF16, align_bytes=64)
+            x_t_words = x_t[:].bitcast(F32)
+            banks = []
+            for p in range(HOPS):
+                bank = flipped.tile([P, 2, P], F32, name="bank")
+                for u in range(2):
+                    words = slice(p * WORDS + u, (p + 1) * WORDS, 2)
+                    nc.tensor.transpose(bank[:, u, :], x_words[:, words], identity[:])
+                banks.append(bank)
+            for p in range(HOPS):
+                copy_out(
+                    out=x_t_words[:, p * 2 * P : (p + 1) * 2 * P].rearrange(
+                        "q (n u) -> q n u", u=2
+                    ),
+                    in_=banks[p][:].rearrange("q u n -> q n u"),
+                )
+            turned[i] = x_t
+
+        def quantise_tile(i):
+            x_t = turned[i]
+            x_codes = operands.tile([P, HOPS * P], U32, align_bytes=64)
+            x_scales = operands.tile([P, HOPS * P], U8, align_bytes=64)
+            n_codes = operands.tile([P, HOPS * P], U32, align_bytes=64)
+            n_scales = operands.tile([P, HOPS * P], U8, align_bytes=64)
+
+            def quantise_x(p):
+                nc.vector.quantize_mx(
+                    out=x_codes[:, p * P : (p + 1) * P].bitcast(FP8X4),
+                    scales=x_scales[:, p * P : (p + 1) * P],
+                    in_=x_t[:, p * width : (p + 1) * width],
+                )
+
+            quantise_x(0)
+            quantise_x(1)
+            half = work.tile([P, HOPS, width], BF16)
+            nc.vector.tensor_scalar(
+                out=half[:].rearrange("q p w -> q (p w)"),
+                in0=x_t[:],
+                scalar1=0.5,
+                scalar2=None,
+                op0=MULT,
+            )
+            quantise_x(2)
+            neigh = work.tile([P, HOPS, width], BF16, align_bytes=64)
+            nc.vector.tensor_tensor(
+                out=neigh[:, 0:2, :], in0=half[:, 0:2, :], in1=half[:, 1:3, :], op=ADD
+            )
+            nc.vector.tensor_tensor(
+                out=neigh[:, 2, :], in0=half[:, 2, :], in1=half[:, 0, :], op=ADD
+            )
+            for s in range(HOPS):
+                nc.vector.quantize_mx(
+                    out=n_codes[:, s * P : (s + 1) * P].bitcast(FP8X4),
+                    scales=n_scales[:, s * P : (s + 1) * P],
+                    in_=neigh[:, s, :],
+                )
+            prepared[i] = (x_codes, x_scales, n_codes, n_scales)
+
+        def multiply(i, p):
+            x_codes, x_scales, n_codes, n_scales = prepared[i]
+            items = slice(i * P, (i + 1) * P)
+            own = slice(p * P, (p + 1) * P)
+            slot = (p + 1) % HOPS
+            others = slice(slot * P, (slot + 1) * P)
+            result = results.tile([P, E], F32)
+            for c in range(HALVES):
+                cols = slice(c * N_PASS, (c + 1) * N_PASS)
+                acc = sums.tile([P, N_PASS], F32)
+                nc.tensor.matmul_mx(
+                    out=acc[:],
+                    lhsT=x_codes[:, own].bitcast(FP8X4),
+                    lhsT_scale=x_scales[:, own],
+                    rhs=w2a_codes[:, cols].bitcast(FP8X4),
+                    rhs_scale=w2a_scales[:, cols],
+                    start=True,
+                    stop=False,
+                )
+                nc.tensor.matmul_mx(
+                    out=acc[:],
+                    lhsT=n_codes[:, others].bitcast(FP8X4),
+                    lhsT_scale=n_scales[:, others],
+                    rhs=w1a_codes[:, cols].bitcast(FP8X4),
+                    rhs_scale=w1a_scales[:, cols],
+                    start=False,
+                    stop=True,
+                )
+                if i + AHEAD >= TILES and c == 1:
+                    nc.vector.tensor_copy(out=result[:, cols], in_=acc[:])
+                else:
+                    nc.scalar.copy(out=result[:, cols], in_=acc[:])
+                if i == TILES - 1:
+                    nc.sync.dma_start(out=out[items, p, cols], in_=result[:, cols])
+            if i < TILES - 1:
+                nc.sync.dma_start(out=out[items, p, :], in_=result[:])
+
+        turn(0, nc.scalar.copy)
+        quantise_tile(0)
+        for c in range(HALVES):
+            regroup_weight(nc, w2a_raw, w2a_grouped, c)
+        turn(1, nc.scalar.copy)
+        for c in range(HALVES):
+            quantise_weight(nc, w2a_grouped, w2a_codes, w2a_scales, c)
+        for c in range(HALVES):
+            regroup_weight(nc, w1a_raw, w1a_grouped, c)
+        for c in range(HALVES):
+            quantise_weight(nc, w1a_grouped, w1a_codes, w1a_scales, c)
+        quantise_tile(1)
+        turn(AHEAD, nc.vector.tensor_copy)
+
+        for i in range(TILES):
+            multiply(i, 0)
+            if AHEAD < i + AHEAD < TILES:
+                turn(i + AHEAD, nc.vector.tensor_copy)
+            if i + AHEAD < TILES:
+                quantise_tile(i + AHEAD)
+            for p in range(1, HOPS):
+                multiply(i, p)

@@ -10,6 +10,7 @@ U8 = mybir.dt.uint8
 FP8X4 = mybir.dt.float8_e4m3fn_x4
 ADD = mybir.AluOpType.add
 MULT = mybir.AluOpType.mult
+COPY = mybir.ActivationFunctionType.Copy
 
 P = 128
 PACK = 4
@@ -18,33 +19,11 @@ WORDS = K // 2
 TILES = ITEMS // P
 N_PASS = 512
 HALVES = E // N_PASS
-W_CHUNK = 256
+W_SCALAR = 256
 RUN = 4
-AHEAD = 2
+WIDTH = P * PACK
 
 FLOPS = 2 * 2 * ITEMS * HOPS * K * E
-
-
-def load_weight(nc, raw, w):
-    nc.sync.dma_start(out=raw[:], in_=w.rearrange("(q t) c -> q t c", t=PACK))
-
-
-def regroup_weight(nc, raw, grouped, c):
-    for copy, first in ((nc.vector.tensor_copy, c * N_PASS), (nc.scalar.copy, c * N_PASS + W_CHUNK)):
-        cols = slice(first, first + W_CHUNK)
-        copy(
-            out=grouped[:, cols, :].rearrange("q (c i) t -> q c t i", i=RUN),
-            in_=raw[:, :, cols].rearrange("q t (c i) -> q c t i", i=RUN),
-        )
-
-
-def quantise_weight(nc, grouped, codes, scales, c):
-    cols = slice(c * N_PASS, (c + 1) * N_PASS)
-    nc.vector.quantize_mx(
-        out=codes[:, cols].bitcast(FP8X4),
-        scales=scales[:, cols],
-        in_=grouped[:, cols, :].rearrange("q c t -> q (c t)"),
-    )
 
 
 def tile_dogtaitujuanji_pa_kernel(tc, x, w1a, w2a, out):
@@ -52,16 +31,13 @@ def tile_dogtaitujuanji_pa_kernel(tc, x, w1a, w2a, out):
     with ExitStack() as ctx:
         keep = ctx.enter_context(tc.tile_pool(name="keep", bufs=1))
         rows = ctx.enter_context(tc.tile_pool(name="rows", bufs=TILES))
-        turns = ctx.enter_context(tc.tile_pool(name="turns", bufs=AHEAD + 1))
-        work = ctx.enter_context(tc.tile_pool(name="work", bufs=2))
-        operands = ctx.enter_context(tc.tile_pool(name="operands", bufs=AHEAD + 2))
-        results = ctx.enter_context(tc.tile_pool(name="results", bufs=6))
-        flipped = ctx.enter_context(tc.psum_pool(name="flipped", bufs=HOPS))
-        sums = ctx.enter_context(tc.psum_pool(name="sums", bufs=8 - HOPS))
+        turns = ctx.enter_context(tc.tile_pool(name="turns", bufs=4))
+        operands = ctx.enter_context(tc.tile_pool(name="operands", bufs=4))
+        results = ctx.enter_context(tc.tile_pool(name="results", bufs=8))
+        flipped = ctx.enter_context(tc.psum_pool(name="flipped", bufs=3))
+        sums = ctx.enter_context(tc.psum_pool(name="sums", bufs=5))
         ctx.enter_context(tc.manual_schedule())
 
-        w2a_raw = keep.tile([P, PACK, E], BF16)
-        w1a_raw = keep.tile([P, PACK, E], BF16)
         x_rows = []
         for i in range(TILES):
             x_tile = rows.tile([P, HOPS * K], BF16, name="x_tile")
@@ -75,144 +51,207 @@ def tile_dogtaitujuanji_pa_kernel(tc, x, w1a, w2a, out):
                 ),
             )
 
+        raw = {}
+
+        def load_weight(w, name, c):
+            w_raw = keep.tile([P, PACK, N_PASS], BF16, name="raw_%s%d" % (name, c))
+            nc.sync.dma_start(
+                out=w_raw[:],
+                in_=w[:, c * N_PASS : (c + 1) * N_PASS].rearrange("(q t) c -> q t c", t=PACK),
+            )
+            raw[name, c] = w_raw
+
         for p in range(HOPS):
             load_x(0, p, 1)
-        load_weight(nc, w2a_raw, w2a)
+        load_weight(w2a, "own", 0)
+        load_weight(w1a, "others", 0)
         load_x(1, 0, HOPS)
-        load_weight(nc, w1a_raw, w1a)
+        load_weight(w2a, "own", 1)
+        load_weight(w1a, "others", 1)
         for i in range(2, TILES):
             load_x(i, 0, HOPS)
 
         identity = keep.tile([P, P], F32)
         make_identity(nc, identity[:])
 
-        w2a_grouped = keep.tile([P, E, PACK], BF16, align_bytes=64)
-        w1a_grouped = keep.tile([P, E, PACK], BF16, align_bytes=64)
-        w2a_codes = keep.tile([P, E], U32, align_bytes=64)
-        w1a_codes = keep.tile([P, E], U32, align_bytes=64)
-        w2a_scales = keep.tile([P, E], U8, align_bytes=64)
-        w1a_scales = keep.tile([P, E], U8, align_bytes=64)
+        grouped, w_codes, w_scales = {}, {}, {}
 
-        width = P * PACK
-        turned = {}
-        prepared = {}
+        def regroup_weight(name, c):
+            w_grouped = keep.tile(
+                [P, N_PASS, PACK], BF16, name="grouped_%s%d" % (name, c), align_bytes=64
+            )
+            grouped[name, c] = w_grouped
 
-        def turn(i, copy_out):
-            x_words = x_rows[i][:].bitcast(F32)
-            x_t = turns.tile([P, HOPS * width], BF16, align_bytes=64)
-            x_t_words = x_t[:].bitcast(F32)
-            banks = []
-            for p in range(HOPS):
-                bank = flipped.tile([P, 2, P], F32, name="bank")
+            def views(first, last):
+                return (
+                    w_grouped[:, first:last, :].rearrange("q (c i) t -> q c t i", i=RUN),
+                    raw[name, c][:, :, first:last].rearrange("q t (c i) -> q c t i", i=RUN),
+                )
+
+            to, source = views(0, W_SCALAR)
+            if name == "own":
+                nc.scalar.copy(out=to, in_=source)
+            else:
+                nc.scalar.activation(out=to, in_=source, func=COPY, scale=0.5)
+            to, source = views(W_SCALAR, N_PASS)
+            if name == "own":
+                nc.vector.tensor_copy(out=to, in_=source)
+            else:
+                nc.vector.tensor_scalar(out=to, in0=source, scalar1=0.5, scalar2=None, op0=MULT)
+
+        def quantise_weight(name, c):
+            codes = keep.tile([P, N_PASS], U32, name="codes_%s%d" % (name, c), align_bytes=64)
+            scales = keep.tile([P, N_PASS], U8, name="scales_%s%d" % (name, c), align_bytes=64)
+            nc.vector.quantize_mx(
+                out=codes[:].bitcast(FP8X4),
+                scales=scales[:],
+                in_=grouped[name, c][:].rearrange("q c t -> q (c t)"),
+            )
+            w_codes[name, c], w_scales[name, c] = codes, scales
+
+        banks, values, codes_of, scales_of = {}, {}, {}, {}
+
+        def transpose(tiles):
+            for h, (i, p) in enumerate((i, p) for i in tiles for p in range(HOPS)):
+                x_words = x_rows[i][:].bitcast(F32)
+                if h % 2 == 0:
+                    bank = flipped.tile([P, 2, 2, P], F32, name="bank")
+                banks[i, p] = (bank, h % 2)
                 for u in range(2):
                     words = slice(p * WORDS + u, (p + 1) * WORDS, 2)
-                    nc.tensor.transpose(bank[:, u, :], x_words[:, words], identity[:])
-                banks.append(bank)
+                    nc.tensor.transpose(bank[:, h % 2, u, :], x_words[:, words], identity[:])
+
+        def start_values(i):
+            v = turns.tile([P, 2 * HOPS, WIDTH], BF16, name="v", align_bytes=64)
+            values[i] = v
+            codes = operands.tile([P, 2 * HOPS * P], U32, name="codes", align_bytes=64)
+            scales = operands.tile([P, 2 * HOPS * P], U8, name="scales", align_bytes=64)
+            codes_of[i], scales_of[i] = codes, scales
+
+        def take_out(i, first, last, copy):
+            words = values[i][:].rearrange("q s w -> q (s w)").bitcast(F32)
+            bank, half = banks[i, first]
+            copy(
+                out=words[:, first * WORDS : last * WORDS].rearrange(
+                    "q (h n u) -> q h n u", h=last - first, u=2
+                ),
+                in_=bank[:, half : half + last - first, :, :].rearrange("q h u n -> q h n u"),
+            )
+
+        def add_pair(i, step):
+            v = values[i]
+            if step == 0:
+                nc.vector.tensor_tensor(
+                    out=v[:, 3:5, :], in0=v[:, 0:2, :], in1=v[:, 1:3, :], op=ADD
+                )
+            else:
+                nc.vector.tensor_tensor(out=v[:, 5, :], in0=v[:, 2, :], in1=v[:, 0, :], op=ADD)
+
+        def quantise(i, first, last):
+            nc.vector.quantize_mx(
+                out=codes_of[i][:, first * P : last * P].bitcast(FP8X4),
+                scales=scales_of[i][:, first * P : last * P],
+                in_=values[i][:, first:last, :].rearrange("q s w -> q (s w)"),
+            )
+
+        result_of = {}
+
+        def multiply(i, p, c, copy):
+            if (i, p) not in result_of:
+                result = results.tile([P, E], F32, name="result")
+                result_of[i, p] = result
+            result = result_of[i, p]
+            cols = slice(c * N_PASS, (c + 1) * N_PASS)
+            acc = sums.tile([P, N_PASS], F32, name="acc")
+            for name, s in (("own", p), ("others", 3 + (p + 1) % HOPS)):
+                slot = slice(s * P, (s + 1) * P)
+                nc.tensor.matmul_mx(
+                    out=acc[:],
+                    lhsT=codes_of[i][:, slot].bitcast(FP8X4),
+                    lhsT_scale=scales_of[i][:, slot],
+                    rhs=w_codes[name, c][:].bitcast(FP8X4),
+                    rhs_scale=w_scales[name, c][:],
+                    start=(name == "own"),
+                    stop=(name == "others"),
+                )
+            copy(out=result[:, cols], in_=acc[:])
+
+        def store(i, p, first, last):
+            cols = slice(first * N_PASS, last * N_PASS)
+            nc.sync.dma_start(out=out[i * P : (i + 1) * P, p, cols], in_=result_of[i, p][:, cols])
+
+        vec, sca = nc.vector.tensor_copy, nc.scalar.copy
+
+        start_values(0)
+        transpose((0,))
+        take_out(0, 0, 1, sca)
+        take_out(0, 1, 2, vec)
+        take_out(0, 2, 3, sca)
+        quantise(0, 0, 2)
+        add_pair(0, 0)
+        quantise(0, 2, 3)
+        add_pair(0, 1)
+        regroup_weight("own", 0)
+        quantise(0, 3, 5)
+        quantise(0, 5, 6)
+        quantise_weight("own", 0)
+        regroup_weight("others", 0)
+        start_values(1)
+        transpose((1,))
+        take_out(1, 0, 2, sca)
+        take_out(1, 2, 3, sca)
+        quantise_weight("others", 0)
+        add_pair(1, 0)
+        quantise(1, 0, 2)
+        add_pair(1, 1)
+        regroup_weight("own", 1)
+        quantise(1, 2, 4)
+        quantise(1, 4, 6)
+        quantise_weight("own", 1)
+        regroup_weight("others", 1)
+        for p in range(HOPS):
+            multiply(0, p, 0, sca)
+            store(0, p, 0, 1)
+        start_values(2)
+        start_values(3)
+        transpose((2, 3))
+        take_out(2, 0, 2, vec)
+        take_out(2, 2, 3, vec)
+        quantise_weight("others", 1)
+        for p in range(HOPS):
+            multiply(1, p, 0, sca)
+            store(1, p, 0, 1)
+
+        def prepare(i):
+            add_pair(i, 0)
+            add_pair(i, 1)
+            quantise(i, 0, 4)
+            quantise(i, 4, 6)
+
+        prepare(2)
+        take_out(3, 0, 1, vec)
+        take_out(3, 1, 3, vec)
+        prepare(3)
+        for i in range(2):
             for p in range(HOPS):
-                copy_out(
-                    out=x_t_words[:, p * 2 * P : (p + 1) * 2 * P].rearrange(
-                        "q (n u) -> q n u", u=2
-                    ),
-                    in_=banks[p][:].rearrange("q u n -> q n u"),
-                )
-            turned[i] = x_t
+                multiply(i, p, 1, sca)
+                store(i, p, 1, 2)
 
-        def quantise_tile(i):
-            x_t = turned[i]
-            x_codes = operands.tile([P, HOPS * P], U32, align_bytes=64)
-            x_scales = operands.tile([P, HOPS * P], U8, align_bytes=64)
-            n_codes = operands.tile([P, HOPS * P], U32, align_bytes=64)
-            n_scales = operands.tile([P, HOPS * P], U8, align_bytes=64)
-
-            def quantise_x(p):
-                nc.vector.quantize_mx(
-                    out=x_codes[:, p * P : (p + 1) * P].bitcast(FP8X4),
-                    scales=x_scales[:, p * P : (p + 1) * P],
-                    in_=x_t[:, p * width : (p + 1) * width],
-                )
-
-            quantise_x(0)
-            quantise_x(1)
-            half = work.tile([P, HOPS, width], BF16)
-            nc.vector.tensor_scalar(
-                out=half[:].rearrange("q p w -> q (p w)"),
-                in0=x_t[:],
-                scalar1=0.5,
-                scalar2=None,
-                op0=MULT,
-            )
-            quantise_x(2)
-            neigh = work.tile([P, HOPS, width], BF16, align_bytes=64)
-            nc.vector.tensor_tensor(
-                out=neigh[:, 0:2, :], in0=half[:, 0:2, :], in1=half[:, 1:3, :], op=ADD
-            )
-            nc.vector.tensor_tensor(
-                out=neigh[:, 2, :], in0=half[:, 2, :], in1=half[:, 0, :], op=ADD
-            )
-            for s in range(HOPS):
-                nc.vector.quantize_mx(
-                    out=n_codes[:, s * P : (s + 1) * P].bitcast(FP8X4),
-                    scales=n_scales[:, s * P : (s + 1) * P],
-                    in_=neigh[:, s, :],
-                )
-            prepared[i] = (x_codes, x_scales, n_codes, n_scales)
-
-        def multiply(i, p):
-            x_codes, x_scales, n_codes, n_scales = prepared[i]
-            items = slice(i * P, (i + 1) * P)
-            own = slice(p * P, (p + 1) * P)
-            slot = (p + 1) % HOPS
-            others = slice(slot * P, (slot + 1) * P)
-            result = results.tile([P, E], F32)
-            for c in range(HALVES):
-                cols = slice(c * N_PASS, (c + 1) * N_PASS)
-                acc = sums.tile([P, N_PASS], F32)
-                nc.tensor.matmul_mx(
-                    out=acc[:],
-                    lhsT=x_codes[:, own].bitcast(FP8X4),
-                    lhsT_scale=x_scales[:, own],
-                    rhs=w2a_codes[:, cols].bitcast(FP8X4),
-                    rhs_scale=w2a_scales[:, cols],
-                    start=True,
-                    stop=False,
-                )
-                nc.tensor.matmul_mx(
-                    out=acc[:],
-                    lhsT=n_codes[:, others].bitcast(FP8X4),
-                    lhsT_scale=n_scales[:, others],
-                    rhs=w1a_codes[:, cols].bitcast(FP8X4),
-                    rhs_scale=w1a_scales[:, cols],
-                    start=False,
-                    stop=True,
-                )
-                if i + AHEAD >= TILES and c == 1:
-                    nc.vector.tensor_copy(out=result[:, cols], in_=acc[:])
-                else:
-                    nc.scalar.copy(out=result[:, cols], in_=acc[:])
-                if i == TILES - 1:
-                    nc.sync.dma_start(out=out[items, p, cols], in_=result[:, cols])
-            if i < TILES - 1:
-                nc.sync.dma_start(out=out[items, p, :], in_=result[:])
-
-        turn(0, nc.scalar.copy)
-        quantise_tile(0)
-        for c in range(HALVES):
-            regroup_weight(nc, w2a_raw, w2a_grouped, c)
-        turn(1, nc.scalar.copy)
-        for c in range(HALVES):
-            quantise_weight(nc, w2a_grouped, w2a_codes, w2a_scales, c)
-        for c in range(HALVES):
-            regroup_weight(nc, w1a_raw, w1a_grouped, c)
-        for c in range(HALVES):
-            quantise_weight(nc, w1a_grouped, w1a_codes, w1a_scales, c)
-        quantise_tile(1)
-        turn(AHEAD, nc.vector.tensor_copy)
-
-        for i in range(TILES):
-            multiply(i, 0)
-            if AHEAD < i + AHEAD < TILES:
-                turn(i + AHEAD, nc.vector.tensor_copy)
-            if i + AHEAD < TILES:
-                quantise_tile(i + AHEAD)
-            for p in range(1, HOPS):
-                multiply(i, p)
+        for i in range(2, TILES):
+            for p in range(HOPS):
+                for c in range(HALVES):
+                    multiply(i, p, c, vec if i == TILES - 1 and c == 1 else sca)
+                    if i == TILES - 1:
+                        store(i, p, c, c + 1)
+                if i < TILES - 1:
+                    store(i, p, 0, 2)
+                if i % 2 == 0 and p == 0 and i + 2 < TILES:
+                    start_values(i + 2)
+                    start_values(i + 3)
+                    transpose((i + 2, i + 3))
+                    take_out(i + 2, 0, 2, vec)
+                    take_out(i + 2, 2, 3, vec)
+                    take_out(i + 3, 0, 1, vec)
+                    take_out(i + 3, 1, 3, vec)
+                    prepare(i + 2)
+                    prepare(i + 3)

@@ -33,6 +33,7 @@ def tile_dogtaitujuanji_pa_kernel(tc, x, w1a, w2a, out):
         rows = ctx.enter_context(tc.tile_pool(name="rows", bufs=TILES))
         turns = ctx.enter_context(tc.tile_pool(name="turns", bufs=4))
         operands = ctx.enter_context(tc.tile_pool(name="operands", bufs=4))
+        splits = ctx.enter_context(tc.tile_pool(name="splits", bufs=2))
         results = ctx.enter_context(tc.tile_pool(name="results", bufs=8))
         flipped = ctx.enter_context(tc.psum_pool(name="flipped", bufs=3))
         sums = ctx.enter_context(tc.psum_pool(name="sums", bufs=5))
@@ -111,6 +112,15 @@ def tile_dogtaitujuanji_pa_kernel(tc, x, w1a, w2a, out):
 
         banks, values, codes_of, scales_of = {}, {}, {}, {}
 
+        split = {}
+
+        def split_words(i):
+            s = splits.tile([P, HOPS, 2, P], F32, name="s")
+            nc.vector.tensor_copy(
+                out=s[:], in_=x_rows[i][:].bitcast(F32).rearrange("n (h j u) -> n h u j", h=HOPS, u=2)
+            )
+            split[i] = s
+
         def transpose(tiles):
             for h, (i, p) in enumerate((i, p) for i in tiles for p in range(HOPS)):
                 x_words = x_rows[i][:].bitcast(F32)
@@ -118,8 +128,11 @@ def tile_dogtaitujuanji_pa_kernel(tc, x, w1a, w2a, out):
                     bank = flipped.tile([P, 2, 2, P], F32, name="bank")
                 banks[i, p] = (bank, h % 2)
                 for u in range(2):
-                    words = slice(p * WORDS + u, (p + 1) * WORDS, 2)
-                    nc.tensor.transpose(bank[:, h % 2, u, :], x_words[:, words], identity[:])
+                    if i in split:
+                        words = split[i][:, p, u, :]
+                    else:
+                        words = x_words[:, p * WORDS + u : (p + 1) * WORDS : 2]
+                    nc.tensor.transpose(bank[:, h % 2, u, :], words, identity[:])
 
         def start_values(i):
             v = turns.tile([P, 2 * HOPS, WIDTH], BF16, name="v", align_bytes=64)
@@ -213,8 +226,7 @@ def tile_dogtaitujuanji_pa_kernel(tc, x, w1a, w2a, out):
             multiply(0, p, 0, sca)
             store(0, p, 0, 1)
         start_values(2)
-        start_values(3)
-        transpose((2, 3))
+        transpose((2,))
         take_out(2, 0, 2, vec)
         take_out(2, 2, 3, vec)
         quantise_weight("others", 1)
@@ -229,9 +241,13 @@ def tile_dogtaitujuanji_pa_kernel(tc, x, w1a, w2a, out):
             quantise(i, 4, 6)
 
         prepare(2)
-        take_out(3, 0, 1, vec)
-        take_out(3, 1, 3, vec)
+        start_values(3)
+        transpose((3,))
+        take_out(3, 0, 2, vec)
+        take_out(3, 2, 3, vec)
         prepare(3)
+        split_words(4)
+        split_words(5)
         for i in range(2):
             for p in range(HOPS):
                 multiply(i, p, 1, sca)
@@ -245,7 +261,7 @@ def tile_dogtaitujuanji_pa_kernel(tc, x, w1a, w2a, out):
                         store(i, p, c, c + 1)
                 if i < TILES - 1:
                     store(i, p, 0, 2)
-                if i % 2 == 0 and p == 0 and i + 2 < TILES:
+                if i % 2 == 0 and p == 1 and i + 2 < TILES:
                     start_values(i + 2)
                     start_values(i + 3)
                     transpose((i + 2, i + 3))
@@ -255,3 +271,6 @@ def tile_dogtaitujuanji_pa_kernel(tc, x, w1a, w2a, out):
                     take_out(i + 3, 1, 3, vec)
                     prepare(i + 2)
                     prepare(i + 3)
+                    if i + 4 < TILES:
+                        split_words(i + 4)
+                        split_words(i + 5)

@@ -30,27 +30,27 @@ def tile_dogtaitujuanji_pa_kernel(tc, x, w1a, w2a, out):
     nc = tc.nc
     with ExitStack() as ctx:
         keep = ctx.enter_context(tc.tile_pool(name="keep", bufs=1))
-        rows = ctx.enter_context(tc.tile_pool(name="rows", bufs=TILES))
+        rows = ctx.enter_context(tc.tile_pool(name="rows", bufs=TILES // 2))
         turns = ctx.enter_context(tc.tile_pool(name="turns", bufs=4))
         operands = ctx.enter_context(tc.tile_pool(name="operands", bufs=4))
         splits = ctx.enter_context(tc.tile_pool(name="splits", bufs=2))
-        results = ctx.enter_context(tc.tile_pool(name="results", bufs=8))
+        halves = ctx.enter_context(tc.tile_pool(name="halves", bufs=4))
+        results = ctx.enter_context(tc.tile_pool(name="results", bufs=4))
         flipped = ctx.enter_context(tc.psum_pool(name="flipped", bufs=3))
         sums = ctx.enter_context(tc.psum_pool(name="sums", bufs=5))
         ctx.enter_context(tc.manual_schedule())
 
-        x_rows = []
-        for i in range(TILES):
-            x_tile = rows.tile([P, HOPS * K], BF16, name="x_tile")
-            x_rows.append(x_tile)
+        x_by_tile = x.rearrange("(n j) h k -> n j (h k)", j=TILES)
+        out_by_tile = out.rearrange("(n j) h e -> n j h e", j=TILES)
+        x_rows, pairs = [], {}
+        for i in range(0, TILES, 2):
+            x_pair = rows.tile([P, 2, HOPS * K], BF16, name="x_pair")
+            x_rows += [x_pair[:, 0, :], x_pair[:, 1, :]]
+            pairs[i] = x_pair
 
         def load_x(i, first_hop, hops):
-            nc.sync.dma_start(
-                out=x_rows[i][:, first_hop * K : (first_hop + hops) * K],
-                in_=x[i * P : (i + 1) * P, first_hop : first_hop + hops, :].rearrange(
-                    "n p k -> n (p k)"
-                ),
-            )
+            words = slice(first_hop * K, (first_hop + hops) * K)
+            nc.sync.dma_start(out=x_rows[i][:, words], in_=x_by_tile[:, i, words])
 
         raw = {}
 
@@ -62,15 +62,17 @@ def tile_dogtaitujuanji_pa_kernel(tc, x, w1a, w2a, out):
             )
             raw[name, c] = w_raw
 
-        for p in range(HOPS):
-            load_x(0, p, 1)
+        load_x(0, 0, 1)
+        load_x(0, 1, 2)
         load_weight(w2a, "own", 0)
         load_weight(w1a, "others", 0)
         load_x(1, 0, HOPS)
         load_weight(w2a, "own", 1)
         load_weight(w1a, "others", 1)
-        for i in range(2, TILES):
-            load_x(i, 0, HOPS)
+        load_x(2, 0, HOPS)
+        load_x(3, 0, HOPS)
+        for i in range(4, TILES, 2):
+            nc.sync.dma_start(out=pairs[i][:], in_=x_by_tile[:, i : i + 2, :])
 
         identity = keep.tile([P, P], F32)
         make_identity(nc, identity[:])
@@ -117,13 +119,13 @@ def tile_dogtaitujuanji_pa_kernel(tc, x, w1a, w2a, out):
         def split_words(i):
             s = splits.tile([P, HOPS, 2, P], F32, name="s")
             nc.vector.tensor_copy(
-                out=s[:], in_=x_rows[i][:].bitcast(F32).rearrange("n (h j u) -> n h u j", h=HOPS, u=2)
+                out=s[:], in_=x_rows[i].bitcast(F32).rearrange("n (h j u) -> n h u j", h=HOPS, u=2)
             )
             split[i] = s
 
         def transpose(tiles):
             for h, (i, p) in enumerate((i, p) for i in tiles for p in range(HOPS)):
-                x_words = x_rows[i][:].bitcast(F32)
+                x_words = x_rows[i].bitcast(F32)
                 if h % 2 == 0:
                     bank = flipped.tile([P, 2, 2, P], F32, name="bank")
                 banks[i, p] = (bank, h % 2)
@@ -170,11 +172,16 @@ def tile_dogtaitujuanji_pa_kernel(tc, x, w1a, w2a, out):
         result_of = {}
 
         def multiply(i, p, c, copy):
-            if (i, p) not in result_of:
-                result = results.tile([P, E], F32, name="result")
-                result_of[i, p] = result
-            result = result_of[i, p]
-            cols = slice(c * N_PASS, (c + 1) * N_PASS)
+            if i < 2:
+                if p == 0:
+                    half = halves.tile([P, HOPS, N_PASS], F32, name="half")
+                    result_of[i, c] = half
+                to = result_of[i, c][:, p, :]
+            else:
+                if p == 0 and c == 0:
+                    result = results.tile([P, HOPS, E], F32, name="result")
+                    result_of[i] = result
+                to = result_of[i][:, p, c * N_PASS : (c + 1) * N_PASS]
             acc = sums.tile([P, N_PASS], F32, name="acc")
             for name, s in (("own", p), ("others", 3 + (p + 1) % HOPS)):
                 slot = slice(s * P, (s + 1) * P)
@@ -187,11 +194,15 @@ def tile_dogtaitujuanji_pa_kernel(tc, x, w1a, w2a, out):
                     start=(name == "own"),
                     stop=(name == "others"),
                 )
-            copy(out=result[:, cols], in_=acc[:])
+            copy(out=to, in_=acc[:])
 
-        def store(i, p, first, last):
+        def store_half(i, c):
+            cols = slice(c * N_PASS, (c + 1) * N_PASS)
+            nc.sync.dma_start(out=out_by_tile[:, i, :, cols], in_=result_of[i, c][:])
+
+        def store(i, p, first=0, last=HALVES):
             cols = slice(first * N_PASS, last * N_PASS)
-            nc.sync.dma_start(out=out[i * P : (i + 1) * P, p, cols], in_=result_of[i, p][:, cols])
+            nc.sync.dma_start(out=out_by_tile[:, i, p, cols], in_=result_of[i][:, p, cols])
 
         vec, sca = nc.vector.tensor_copy, nc.scalar.copy
 
@@ -224,7 +235,7 @@ def tile_dogtaitujuanji_pa_kernel(tc, x, w1a, w2a, out):
         regroup_weight("others", 1)
         for p in range(HOPS):
             multiply(0, p, 0, sca)
-            store(0, p, 0, 1)
+        store_half(0, 0)
         start_values(2)
         transpose((2,))
         take_out(2, 0, 2, vec)
@@ -232,7 +243,7 @@ def tile_dogtaitujuanji_pa_kernel(tc, x, w1a, w2a, out):
         quantise_weight("others", 1)
         for p in range(HOPS):
             multiply(1, p, 0, sca)
-            store(1, p, 0, 1)
+        store_half(1, 0)
 
         def prepare(i):
             add_pair(i, 0)
@@ -251,16 +262,16 @@ def tile_dogtaitujuanji_pa_kernel(tc, x, w1a, w2a, out):
         for i in range(2):
             for p in range(HOPS):
                 multiply(i, p, 1, sca)
-                store(i, p, 1, 2)
+            store_half(i, 1)
 
         for i in range(2, TILES):
             for p in range(HOPS):
                 for c in range(HALVES):
                     multiply(i, p, c, vec if i == TILES - 1 and c == 1 else sca)
-                    if i == TILES - 1:
+                    if i == TILES - 1 and p == HOPS - 1:
                         store(i, p, c, c + 1)
-                if i < TILES - 1:
-                    store(i, p, 0, 2)
+                if i < TILES - 1 or p < HOPS - 1:
+                    store(i, p)
                 if i % 2 == 0 and p == 1 and i + 2 < TILES:
                     start_values(i + 2)
                     start_values(i + 3)

@@ -267,7 +267,8 @@ def tile_dogtaitujuanji_pa_kernel(tc, x, w1a, w2a, out):
         for i in range(2, TILES):
             for p in range(HOPS):
                 for c in range(HALVES):
-                    multiply(i, p, c, vec if i == TILES - 1 and c == 1 else sca)
+                    by_vector = c == 1 and (i >= TILES - 2 or (i % 2 == 0 and p < 2))
+                    multiply(i, p, c, vec if by_vector else sca)
                     if i == TILES - 1 and p == HOPS - 1:
                         store(i, p, c, c + 1)
                 if i < TILES - 1 or p < HOPS - 1:

@@ -62,20 +62,23 @@ def tile_dogtaitujuanji_pa_kernel(tc, x, w1a, w2a, out):
             )
             raw[name, c] = w_raw
 
-        load_x(0, 0, 1)
-        load_x(0, 1, 2)
+        for p in range(HOPS):
+            load_x(0, p, 1)
         load_weight(w2a, "own", 0)
-        load_weight(w1a, "others", 0)
         load_x(1, 0, HOPS)
+        load_weight(w1a, "others", 0)
+        load_x(2, 0, HOPS)
         load_weight(w2a, "own", 1)
         load_weight(w1a, "others", 1)
-        load_x(2, 0, HOPS)
         load_x(3, 0, HOPS)
         for i in range(4, TILES, 2):
             nc.sync.dma_start(out=pairs[i][:], in_=x_by_tile[:, i : i + 2, :])
 
         identity = keep.tile([P, P], F32)
         make_identity(nc, identity[:])
+        zero_tile = keep.tile([P, N_PASS], BF16)
+        nc.vector.memset(zero_tile[:], 0.0)
+        zeros = zero_tile[:]
 
         grouped, w_codes, w_scales = {}, {}, {}
 
@@ -123,18 +126,19 @@ def tile_dogtaitujuanji_pa_kernel(tc, x, w1a, w2a, out):
             )
             split[i] = s
 
-        def transpose(tiles):
+        def transpose(tiles, hops_per_bank=2):
             for h, (i, p) in enumerate((i, p) for i in tiles for p in range(HOPS)):
                 x_words = x_rows[i].bitcast(F32)
-                if h % 2 == 0:
+                half = h % hops_per_bank
+                if half == 0:
                     bank = flipped.tile([P, 2, 2, P], F32, name="bank")
-                banks[i, p] = (bank, h % 2)
+                banks[i, p] = (bank, half)
                 for u in range(2):
                     if i in split:
                         words = split[i][:, p, u, :]
                     else:
                         words = x_words[:, p * WORDS + u : (p + 1) * WORDS : 2]
-                    nc.tensor.transpose(bank[:, h % 2, u, :], words, identity[:])
+                    nc.tensor.transpose(bank[:, half, u, :], words, identity[:])
 
         def start_values(i):
             v = turns.tile([P, 2 * HOPS, WIDTH], BF16, name="v", align_bytes=64)
@@ -168,6 +172,11 @@ def tile_dogtaitujuanji_pa_kernel(tc, x, w1a, w2a, out):
                 scales=scales_of[i][:, first * P : last * P],
                 in_=values[i][:, first:last, :].rearrange("q s w -> q (s w)"),
             )
+
+        def warm(moving, count):
+            for n in range(count):
+                acc = sums.tile([P, N_PASS], F32, name="acc")
+                nc.tensor.matmul(acc[:], lhsT=zero_tile[:, 0:P], rhs=moving, start=True, stop=True)
 
         result_of = {}
 
@@ -207,11 +216,15 @@ def tile_dogtaitujuanji_pa_kernel(tc, x, w1a, w2a, out):
         vec, sca = nc.vector.tensor_copy, nc.scalar.copy
 
         start_values(0)
-        transpose((0,))
+        warm(zeros, 4)
+        transpose((0,), 1)
         take_out(0, 0, 1, sca)
         take_out(0, 1, 2, vec)
         take_out(0, 2, 3, sca)
-        quantise(0, 0, 2)
+        warm(zeros, 2)
+        warm(raw["own", 0][:, 0, :], 2)
+        quantise(0, 0, 1)
+        quantise(0, 1, 2)
         add_pair(0, 0)
         quantise(0, 2, 3)
         add_pair(0, 1)
@@ -219,25 +232,27 @@ def tile_dogtaitujuanji_pa_kernel(tc, x, w1a, w2a, out):
         quantise(0, 3, 5)
         quantise(0, 5, 6)
         quantise_weight("own", 0)
-        regroup_weight("others", 0)
         start_values(1)
         transpose((1,))
         take_out(1, 0, 2, sca)
         take_out(1, 2, 3, sca)
-        quantise_weight("others", 0)
+        warm(raw["others", 0][:, 0, :], 2)
+        regroup_weight("others", 0)
         add_pair(1, 0)
         quantise(1, 0, 2)
-        add_pair(1, 1)
-        regroup_weight("own", 1)
-        quantise(1, 2, 4)
-        quantise(1, 4, 6)
-        quantise_weight("own", 1)
-        regroup_weight("others", 1)
-        for p in range(HOPS):
-            multiply(0, p, 0, sca)
-        store_half(0, 0)
+        quantise_weight("others", 0)
         start_values(2)
         transpose((2,))
+        add_pair(1, 1)
+        quantise(1, 2, 4)
+        quantise(1, 4, 6)
+        regroup_weight("own", 1)
+        multiply(0, 0, 0, sca)
+        quantise_weight("own", 1)
+        regroup_weight("others", 1)
+        multiply(0, 1, 0, sca)
+        multiply(0, 2, 0, sca)
+        store_half(0, 0)
         take_out(2, 0, 2, vec)
         take_out(2, 2, 3, vec)
         quantise_weight("others", 1)

@@ -33,7 +33,7 @@ def tile_dogtaitujuanji_pa_kernel(tc, x, w1a, w2a, out):
         rows = ctx.enter_context(tc.tile_pool(name="rows", bufs=TILES // 2))
         turns = ctx.enter_context(tc.tile_pool(name="turns", bufs=4))
         operands = ctx.enter_context(tc.tile_pool(name="operands", bufs=4))
-        splits = ctx.enter_context(tc.tile_pool(name="splits", bufs=2))
+        splits = ctx.enter_context(tc.tile_pool(name="splits", bufs=4))
         halves = ctx.enter_context(tc.tile_pool(name="halves", bufs=4))
         results = ctx.enter_context(tc.tile_pool(name="results", bufs=4))
         flipped = ctx.enter_context(tc.psum_pool(name="flipped", bufs=3))
@@ -82,7 +82,7 @@ def tile_dogtaitujuanji_pa_kernel(tc, x, w1a, w2a, out):
 
         grouped, w_codes, w_scales = {}, {}, {}
 
-        def regroup_weight(name, c):
+        def regroup_weight(name, c, by_scalar=W_SCALAR):
             w_grouped = keep.tile(
                 [P, N_PASS, PACK], BF16, name="grouped_%s%d" % (name, c), align_bytes=64
             )
@@ -94,12 +94,12 @@ def tile_dogtaitujuanji_pa_kernel(tc, x, w1a, w2a, out):
                     raw[name, c][:, :, first:last].rearrange("q t (c i) -> q c t i", i=RUN),
                 )
 
-            to, source = views(0, W_SCALAR)
+            to, source = views(0, by_scalar)
             if name == "own":
                 nc.scalar.copy(out=to, in_=source)
             else:
                 nc.scalar.activation(out=to, in_=source, func=COPY, scale=0.5)
-            to, source = views(W_SCALAR, N_PASS)
+            to, source = views(by_scalar, N_PASS)
             if name == "own":
                 nc.vector.tensor_copy(out=to, in_=source)
             else:
@@ -119,9 +119,9 @@ def tile_dogtaitujuanji_pa_kernel(tc, x, w1a, w2a, out):
 
         split = {}
 
-        def split_words(i):
+        def split_words(i, copy):
             s = splits.tile([P, HOPS, 2, P], F32, name="s")
-            nc.vector.tensor_copy(
+            copy(
                 out=s[:], in_=x_rows[i].bitcast(F32).rearrange("n (h j u) -> n h u j", h=HOPS, u=2)
             )
             split[i] = s
@@ -180,6 +180,25 @@ def tile_dogtaitujuanji_pa_kernel(tc, x, w1a, w2a, out):
 
         result_of = {}
 
+        banks_open = {}
+
+        def first_pass(i, p, c):
+            acc = sums.tile([P, N_PASS], F32, name="acc")
+            banks_open[i, p, c] = acc
+            one_pass(i, p, c, "own", p)
+
+        def one_pass(i, p, c, name, s):
+            slot = slice(s * P, (s + 1) * P)
+            nc.tensor.matmul_mx(
+                out=banks_open[i, p, c][:],
+                lhsT=codes_of[i][:, slot].bitcast(FP8X4),
+                lhsT_scale=scales_of[i][:, slot],
+                rhs=w_codes[name, c][:].bitcast(FP8X4),
+                rhs_scale=w_scales[name, c][:],
+                start=(name == "own"),
+                stop=(name == "others"),
+            )
+
         def multiply(i, p, c, copy):
             if i < 2:
                 if p == 0:
@@ -191,19 +210,10 @@ def tile_dogtaitujuanji_pa_kernel(tc, x, w1a, w2a, out):
                     result = results.tile([P, HOPS, E], F32, name="result")
                     result_of[i] = result
                 to = result_of[i][:, p, c * N_PASS : (c + 1) * N_PASS]
-            acc = sums.tile([P, N_PASS], F32, name="acc")
-            for name, s in (("own", p), ("others", 3 + (p + 1) % HOPS)):
-                slot = slice(s * P, (s + 1) * P)
-                nc.tensor.matmul_mx(
-                    out=acc[:],
-                    lhsT=codes_of[i][:, slot].bitcast(FP8X4),
-                    lhsT_scale=scales_of[i][:, slot],
-                    rhs=w_codes[name, c][:].bitcast(FP8X4),
-                    rhs_scale=w_scales[name, c][:],
-                    start=(name == "own"),
-                    stop=(name == "others"),
-                )
-            copy(out=to, in_=acc[:])
+            if (i, p, c) not in banks_open:
+                first_pass(i, p, c)
+            one_pass(i, p, c, "others", 3 + (p + 1) % HOPS)
+            copy(out=to, in_=banks_open[i, p, c][:])
 
         def store_half(i, c):
             cols = slice(c * N_PASS, (c + 1) * N_PASS)
@@ -216,7 +226,7 @@ def tile_dogtaitujuanji_pa_kernel(tc, x, w1a, w2a, out):
         vec, sca = nc.vector.tensor_copy, nc.scalar.copy
 
         start_values(0)
-        warm(zeros, 4)
+        warm(zeros, 2)
         transpose((0,), 1)
         take_out(0, 0, 1, sca)
         take_out(0, 1, 2, vec)
@@ -236,25 +246,26 @@ def tile_dogtaitujuanji_pa_kernel(tc, x, w1a, w2a, out):
         transpose((1,))
         take_out(1, 0, 2, sca)
         take_out(1, 2, 3, sca)
-        warm(raw["others", 0][:, 0, :], 2)
+        for p in range(HOPS):
+            first_pass(0, p, 0)
         regroup_weight("others", 0)
         add_pair(1, 0)
         quantise(1, 0, 2)
         quantise_weight("others", 0)
         start_values(2)
         transpose((2,))
+        take_out(2, 0, 2, sca)
+        take_out(2, 2, 3, sca)
         add_pair(1, 1)
         quantise(1, 2, 4)
         quantise(1, 4, 6)
         regroup_weight("own", 1)
         multiply(0, 0, 0, sca)
         quantise_weight("own", 1)
-        regroup_weight("others", 1)
+        regroup_weight("others", 1, 128)
         multiply(0, 1, 0, sca)
         multiply(0, 2, 0, sca)
         store_half(0, 0)
-        take_out(2, 0, 2, vec)
-        take_out(2, 2, 3, vec)
         quantise_weight("others", 1)
         for p in range(HOPS):
             multiply(1, p, 0, sca)
@@ -272,8 +283,8 @@ def tile_dogtaitujuanji_pa_kernel(tc, x, w1a, w2a, out):
         take_out(3, 0, 2, vec)
         take_out(3, 2, 3, vec)
         prepare(3)
-        split_words(4)
-        split_words(5)
+        split_words(4, vec)
+        split_words(5, vec)
         for i in range(2):
             for p in range(HOPS):
                 multiply(i, p, 1, sca)
@@ -292,12 +303,12 @@ def tile_dogtaitujuanji_pa_kernel(tc, x, w1a, w2a, out):
                     start_values(i + 2)
                     start_values(i + 3)
                     transpose((i + 2, i + 3))
+                    if i + 4 < TILES:
+                        split_words(i + 4, sca)
+                        split_words(i + 5, sca)
                     take_out(i + 2, 0, 2, vec)
                     take_out(i + 2, 2, 3, vec)
                     take_out(i + 3, 0, 1, vec)
                     take_out(i + 3, 1, 3, vec)
                     prepare(i + 2)
                     prepare(i + 3)
-                    if i + 4 < TILES:
-                        split_words(i + 4)
-                        split_words(i + 5)

@@ -18,6 +18,7 @@ ITEMS, HOPS, K, E = 1024, 3, 512, 1024
 WORDS = K // 2
 TILES = ITEMS // P
 N_PASS = 512
+N_LAST = 256
 HALVES = E // N_PASS
 W_SCALAR = 256
 RUN = 4
@@ -219,14 +220,13 @@ def tile_dogtaitujuanji_pa_kernel(tc, x, w1a, w2a, out):
             cols = slice(c * N_PASS, (c + 1) * N_PASS)
             nc.sync.dma_start(out=out_by_tile[:, i, :, cols], in_=result_of[i, c][:])
 
-        def store(i, p, first=0, last=HALVES):
-            cols = slice(first * N_PASS, last * N_PASS)
+        def store(i, p, cols):
             nc.sync.dma_start(out=out_by_tile[:, i, p, cols], in_=result_of[i][:, p, cols])
 
         vec, sca = nc.vector.tensor_copy, nc.scalar.copy
 
         start_values(0)
-        warm(zeros, 2)
+        warm(zeros, 3)
         transpose((0,), 1)
         take_out(0, 0, 1, sca)
         take_out(0, 1, 2, vec)
@@ -246,6 +246,7 @@ def tile_dogtaitujuanji_pa_kernel(tc, x, w1a, w2a, out):
         transpose((1,))
         take_out(1, 0, 2, sca)
         take_out(1, 2, 3, sca)
+        warm(zeros, 2)
         for p in range(HOPS):
             first_pass(0, p, 0)
         regroup_weight("others", 0)
@@ -293,13 +294,15 @@ def tile_dogtaitujuanji_pa_kernel(tc, x, w1a, w2a, out):
         for i in range(2, TILES):
             for p in range(HOPS):
                 for c in range(HALVES):
+                    if (i, p, c) == (TILES - 1, HOPS - 1, HALVES - 1):
+                        break
                     by_vector = c == 1 and (i >= TILES - 2 or (i % 2 == 0 and p < 2))
                     multiply(i, p, c, vec if by_vector else sca)
-                    if i == TILES - 1 and p == HOPS - 1:
-                        store(i, p, c, c + 1)
-                if i < TILES - 1 or p < HOPS - 1:
-                    store(i, p)
-                if i % 2 == 0 and p == 1 and i + 2 < TILES:
+                if (i, p) == (TILES - 1, HOPS - 1):
+                    store(i, p, slice(0, N_PASS))
+                else:
+                    store(i, p, slice(0, E))
+                if i % 2 == 0 and p == 2 and i + 2 < TILES:
                     start_values(i + 2)
                     start_values(i + 3)
                     transpose((i + 2, i + 3))
@@ -312,3 +315,22 @@ def tile_dogtaitujuanji_pa_kernel(tc, x, w1a, w2a, out):
                     take_out(i + 3, 1, 3, vec)
                     prepare(i + 2)
                     prepare(i + 3)
+
+        i, p, c = TILES - 1, HOPS - 1, HALVES - 1
+        for first, copy in ((0, vec), (N_LAST, sca)):
+            acc = sums.tile([P, N_LAST], F32, name="acc")
+            part = slice(first, first + N_LAST)
+            for name, s in (("own", p), ("others", 3 + (p + 1) % HOPS)):
+                slot = slice(s * P, (s + 1) * P)
+                nc.tensor.matmul_mx(
+                    out=acc[:],
+                    lhsT=codes_of[i][:, slot].bitcast(FP8X4),
+                    lhsT_scale=scales_of[i][:, slot],
+                    rhs=w_codes[name, c][:, part].bitcast(FP8X4),
+                    rhs_scale=w_scales[name, c][:, part],
+                    start=(name == "own"),
+                    stop=(name == "others"),
+                )
+            cols = slice(c * N_PASS + first, c * N_PASS + first + N_LAST)
+            copy(out=result_of[i][:, p, cols], in_=acc[:])
+            store(i, p, cols)

@@ -216,9 +216,9 @@ def tile_dogtaitujuanji_pa_kernel(tc, x, w1a, w2a, out):
             one_pass(i, p, c, "others", 3 + (p + 1) % HOPS)
             copy(out=to, in_=banks_open[i, p, c][:])
 
-        def store_half(i, c):
+        def store_half(i, c, hops=slice(0, HOPS)):
             cols = slice(c * N_PASS, (c + 1) * N_PASS)
-            nc.sync.dma_start(out=out_by_tile[:, i, :, cols], in_=result_of[i, c][:])
+            nc.sync.dma_start(out=out_by_tile[:, i, hops, cols], in_=result_of[i, c][:, hops, :])
 
         def store(i, p, cols):
             nc.sync.dma_start(out=out_by_tile[:, i, p, cols], in_=result_of[i][:, p, cols])
@@ -257,16 +257,19 @@ def tile_dogtaitujuanji_pa_kernel(tc, x, w1a, w2a, out):
         transpose((2,))
         take_out(2, 0, 2, sca)
         take_out(2, 2, 3, sca)
+        for p in range(2):
+            first_pass(1, p, 0)
         add_pair(1, 1)
         quantise(1, 2, 4)
         quantise(1, 4, 6)
-        regroup_weight("own", 1)
         multiply(0, 0, 0, sca)
-        quantise_weight("own", 1)
+        store_half(0, 0, slice(0, 1))
+        regroup_weight("own", 1, 192)
         regroup_weight("others", 1, 128)
+        quantise_weight("own", 1)
         multiply(0, 1, 0, sca)
         multiply(0, 2, 0, sca)
-        store_half(0, 0)
+        store_half(0, 0, slice(1, HOPS))
         quantise_weight("others", 1)
         for p in range(HOPS):
             multiply(1, p, 0, sca)
@@ -278,11 +281,14 @@ def tile_dogtaitujuanji_pa_kernel(tc, x, w1a, w2a, out):
             quantise(i, 0, 4)
             quantise(i, 4, 6)
 
-        prepare(2)
         start_values(3)
         transpose((3,))
+        add_pair(2, 0)
+        add_pair(2, 1)
         take_out(3, 0, 2, vec)
         take_out(3, 2, 3, vec)
+        quantise(2, 0, 4)
+        quantise(2, 4, 6)
         prepare(3)
         split_words(4, vec)
         split_words(5, vec)

from contextlib import ExitStack

import concourse.mybir as mybir
from concourse.masks import make_identity

F32 = mybir.dt.float32
BF16 = mybir.dt.bfloat16
U32 = mybir.dt.uint32
U8 = mybir.dt.uint8
FP8X4 = mybir.dt.float8_e4m3fn_x4
ADD = mybir.AluOpType.add
MULT = mybir.AluOpType.mult
COPY = mybir.ActivationFunctionType.Copy

P = 128
PACK = 4
ITEMS, HOPS, K, E = 1024, 3, 512, 1024
WORDS = K // 2
TILES = ITEMS // P
N_PASS = 512
N_LAST = 256
HALVES = E // N_PASS
W_SCALAR = 256
RUN = 4
WIDTH = P * PACK

FLOPS = 2 * 2 * ITEMS * HOPS * K * E


def tile_dogtaitujuanji_pa_kernel(tc, x, w1a, w2a, out):
    nc = tc.nc
    with ExitStack() as ctx:
        keep = ctx.enter_context(tc.tile_pool(name="keep", bufs=1))
        rows = ctx.enter_context(tc.tile_pool(name="rows", bufs=TILES // 2))
        turns = ctx.enter_context(tc.tile_pool(name="turns", bufs=4))
        operands = ctx.enter_context(tc.tile_pool(name="operands", bufs=4))
        splits = ctx.enter_context(tc.tile_pool(name="splits", bufs=4))
        halves = ctx.enter_context(tc.tile_pool(name="halves", bufs=4))
        results = ctx.enter_context(tc.tile_pool(name="results", bufs=4))
        flipped = ctx.enter_context(tc.psum_pool(name="flipped", bufs=3))
        sums = ctx.enter_context(tc.psum_pool(name="sums", bufs=5))
        ctx.enter_context(tc.manual_schedule())

        x_by_tile = x.rearrange("(n j) h k -> n j (h k)", j=TILES)
        out_by_tile = out.rearrange("(n j) h e -> n j h e", j=TILES)
        x_rows, pairs = [], {}
        for i in range(0, TILES, 2):
            x_pair = rows.tile([P, 2, HOPS * K], BF16, name="x_pair")
            x_rows += [x_pair[:, 0, :], x_pair[:, 1, :]]
            pairs[i] = x_pair

        def load_x(i, first_hop, hops):
            words = slice(first_hop * K, (first_hop + hops) * K)
            nc.sync.dma_start(out=x_rows[i][:, words], in_=x_by_tile[:, i, words])

        raw = {}

        def load_weight(w, name, c):
            w_raw = keep.tile([P, PACK, N_PASS], BF16, name="raw_%s%d" % (name, c))
            nc.sync.dma_start(
                out=w_raw[:],
                in_=w[:, c * N_PASS : (c + 1) * N_PASS].rearrange("(q t) c -> q t c", t=PACK),
            )
            raw[name, c] = w_raw

        for p in range(HOPS):
            load_x(0, p, 1)
        load_weight(w2a, "own", 0)
        load_x(1, 0, HOPS)
        load_weight(w1a, "others", 0)
        load_x(2, 0, HOPS)
        load_weight(w2a, "own", 1)
        load_weight(w1a, "others", 1)
        load_x(3, 0, HOPS)
        for i in range(4, TILES, 2):
            nc.sync.dma_start(out=pairs[i][:], in_=x_by_tile[:, i : i + 2, :])

        identity = keep.tile([P, P], F32)
        make_identity(nc, identity[:])
        zero_tile = keep.tile([P, N_PASS], BF16)
        nc.vector.memset(zero_tile[:], 0.0)
        zeros = zero_tile[:]

        grouped, w_codes, w_scales = {}, {}, {}

        def regroup_weight(name, c, by_scalar=W_SCALAR):
            w_grouped = keep.tile(
                [P, N_PASS, PACK], BF16, name="grouped_%s%d" % (name, c), align_bytes=64
            )
            grouped[name, c] = w_grouped

            def views(first, last):
                return (
                    w_grouped[:, first:last, :].rearrange("q (c i) t -> q c t i", i=RUN),
                    raw[name, c][:, :, first:last].rearrange("q t (c i) -> q c t i", i=RUN),
                )

            to, source = views(0, by_scalar)
            if name == "own":
                nc.scalar.copy(out=to, in_=source)
            else:
                nc.scalar.activation(out=to, in_=source, func=COPY, scale=0.5)
            to, source = views(by_scalar, N_PASS)
            if name == "own":
                nc.vector.tensor_copy(out=to, in_=source)
            else:
                nc.vector.tensor_scalar(out=to, in0=source, scalar1=0.5, scalar2=None, op0=MULT)

        def quantise_weight(name, c):
            codes = keep.tile([P, N_PASS], U32, name="codes_%s%d" % (name, c), align_bytes=64)
            scales = keep.tile([P, N_PASS], U8, name="scales_%s%d" % (name, c), align_bytes=64)
            nc.vector.quantize_mx(
                out=codes[:].bitcast(FP8X4),
                scales=scales[:],
                in_=grouped[name, c][:].rearrange("q c t -> q (c t)"),
            )
            w_codes[name, c], w_scales[name, c] = codes, scales

        banks, values, codes_of, scales_of = {}, {}, {}, {}

        split = {}

        def split_words(i, copy):
            s = splits.tile([P, HOPS, 2, P], F32, name="s")
            copy(
                out=s[:], in_=x_rows[i].bitcast(F32).rearrange("n (h j u) -> n h u j", h=HOPS, u=2)
            )
            split[i] = s

        def transpose(tiles, hops_per_bank=2):
            for h, (i, p) in enumerate((i, p) for i in tiles for p in range(HOPS)):
                x_words = x_rows[i].bitcast(F32)
                half = h % hops_per_bank
                if half == 0:
                    bank = flipped.tile([P, 2, 2, P], F32, name="bank")
                banks[i, p] = (bank, half)
                for u in range(2):
                    if i in split:
                        words = split[i][:, p, u, :]
                    else:
                        words = x_words[:, p * WORDS + u : (p + 1) * WORDS : 2]
                    nc.tensor.transpose(bank[:, half, u, :], words, identity[:])

        def start_values(i):
            v = turns.tile([P, 2 * HOPS, WIDTH], BF16, name="v", align_bytes=64)
            values[i] = v
            codes = operands.tile([P, 2 * HOPS * P], U32, name="codes", align_bytes=64)
            scales = operands.tile([P, 2 * HOPS * P], U8, name="scales", align_bytes=64)
            codes_of[i], scales_of[i] = codes, scales

        def take_out(i, first, last, copy):
            words = values[i][:].rearrange("q s w -> q (s w)").bitcast(F32)
            bank, half = banks[i, first]
            copy(
                out=words[:, first * WORDS : last * WORDS].rearrange(
                    "q (h n u) -> q h n u", h=last - first, u=2
                ),
                in_=bank[:, half : half + last - first, :, :].rearrange("q h u n -> q h n u"),
            )

        def add_pair(i, step):
            v = values[i]
            if step == 0:
                nc.vector.tensor_tensor(
                    out=v[:, 3:5, :], in0=v[:, 0:2, :], in1=v[:, 1:3, :], op=ADD
                )
            else:
                nc.vector.tensor_tensor(out=v[:, 5, :], in0=v[:, 2, :], in1=v[:, 0, :], op=ADD)

        def quantise(i, first, last):
            nc.vector.quantize_mx(
                out=codes_of[i][:, first * P : last * P].bitcast(FP8X4),
                scales=scales_of[i][:, first * P : last * P],
                in_=values[i][:, first:last, :].rearrange("q s w -> q (s w)"),
            )

        def warm(moving, count):
            for n in range(count):
                acc = sums.tile([P, N_PASS], F32, name="acc")
                nc.tensor.matmul(acc[:], lhsT=zero_tile[:, 0:P], rhs=moving, start=True, stop=True)

        result_of = {}

        banks_open = {}

        def first_pass(i, p, c):
            acc = sums.tile([P, N_PASS], F32, name="acc")
            banks_open[i, p, c] = acc
            one_pass(i, p, c, "own", p)

        def one_pass(i, p, c, name, s):
            slot = slice(s * P, (s + 1) * P)
            nc.tensor.matmul_mx(
                out=banks_open[i, p, c][:],
                lhsT=codes_of[i][:, slot].bitcast(FP8X4),
                lhsT_scale=scales_of[i][:, slot],
                rhs=w_codes[name, c][:].bitcast(FP8X4),
                rhs_scale=w_scales[name, c][:],
                start=(name == "own"),
                stop=(name == "others"),
            )

        def multiply(i, p, c, copy):
            if i < 2:
                if p == 0:
                    half = halves.tile([P, HOPS, N_PASS], F32, name="half")
                    result_of[i, c] = half
                to = result_of[i, c][:, p, :]
            else:
                if p == 0 and c == 0:
                    result = results.tile([P, HOPS, E], F32, name="result")
                    result_of[i] = result
                to = result_of[i][:, p, c * N_PASS : (c + 1) * N_PASS]
            if (i, p, c) not in banks_open:
                first_pass(i, p, c)
            one_pass(i, p, c, "others", 3 + (p + 1) % HOPS)
            copy(out=to, in_=banks_open[i, p, c][:])

        def store_half(i, c, hops=slice(0, HOPS)):
            cols = slice(c * N_PASS, (c + 1) * N_PASS)
            nc.sync.dma_start(out=out_by_tile[:, i, hops, cols], in_=result_of[i, c][:, hops, :])

        def store(i, p, cols):
            nc.sync.dma_start(out=out_by_tile[:, i, p, cols], in_=result_of[i][:, p, cols])

        vec, sca = nc.vector.tensor_copy, nc.scalar.copy

        start_values(0)
        warm(zeros, 3)
        transpose((0,), 1)
        take_out(0, 0, 1, sca)
        take_out(0, 1, 2, vec)
        take_out(0, 2, 3, sca)
        warm(zeros, 2)
        warm(raw["own", 0][:, 0, :], 2)
        quantise(0, 0, 1)
        quantise(0, 1, 2)
        add_pair(0, 0)
        quantise(0, 2, 3)
        add_pair(0, 1)
        regroup_weight("own", 0)
        quantise(0, 3, 5)
        quantise(0, 5, 6)
        quantise_weight("own", 0)
        start_values(1)
        transpose((1,))
        take_out(1, 0, 2, sca)
        take_out(1, 2, 3, sca)
        warm(zeros, 2)
        for p in range(HOPS):
            first_pass(0, p, 0)
        regroup_weight("others", 0)
        add_pair(1, 0)
        quantise(1, 0, 2)
        quantise_weight("others", 0)
        start_values(2)
        transpose((2,))
        take_out(2, 0, 2, sca)
        take_out(2, 2, 3, sca)
        for p in range(2):
            first_pass(1, p, 0)
        add_pair(1, 1)
        quantise(1, 2, 4)
        quantise(1, 4, 6)
        multiply(0, 0, 0, sca)
        store_half(0, 0, slice(0, 1))
        regroup_weight("own", 1, 192)
        regroup_weight("others", 1, 128)
        quantise_weight("own", 1)
        multiply(0, 1, 0, sca)
        multiply(0, 2, 0, sca)
        store_half(0, 0, slice(1, HOPS))
        quantise_weight("others", 1)
        for p in range(HOPS):
            multiply(1, p, 0, sca)
        store_half(1, 0)

        def prepare(i):
            add_pair(i, 0)
            add_pair(i, 1)
            quantise(i, 0, 4)
            quantise(i, 4, 6)

        start_values(3)
        transpose((3,))
        add_pair(2, 0)
        add_pair(2, 1)
        take_out(3, 0, 2, vec)
        take_out(3, 2, 3, vec)
        quantise(2, 0, 4)
        quantise(2, 4, 6)
        prepare(3)
        split_words(4, vec)
        split_words(5, vec)
        for i in range(2):
            for p in range(HOPS):
                multiply(i, p, 1, sca)
            store_half(i, 1)

        for i in range(2, TILES):
            for p in range(HOPS):
                for c in range(HALVES):
                    if (i, p, c) == (TILES - 1, HOPS - 1, HALVES - 1):
                        break
                    by_vector = c == 1 and (i >= TILES - 2 or (i % 2 == 0 and p < 2))
                    multiply(i, p, c, vec if by_vector else sca)
                if (i, p) == (TILES - 1, HOPS - 1):
                    store(i, p, slice(0, N_PASS))
                else:
                    store(i, p, slice(0, E))
                if i % 2 == 0 and p == 2 and i + 2 < TILES:
                    start_values(i + 2)
                    start_values(i + 3)
                    transpose((i + 2, i + 3))
                    if i + 4 < TILES:
                        split_words(i + 4, sca)
                        split_words(i + 5, sca)
                    take_out(i + 2, 0, 2, vec)
                    take_out(i + 2, 2, 3, vec)
                    take_out(i + 3, 0, 1, vec)
                    take_out(i + 3, 1, 3, vec)
                    prepare(i + 2)
                    prepare(i + 3)

        i, p, c = TILES - 1, HOPS - 1, HALVES - 1
        for first, copy in ((0, vec), (N_LAST, sca)):
            acc = sums.tile([P, N_LAST], F32, name="acc")
            part = slice(first, first + N_LAST)
            for name, s in (("own", p), ("others", 3 + (p + 1) % HOPS)):
                slot = slice(s * P, (s + 1) * P)
                nc.tensor.matmul_mx(
                    out=acc[:],
                    lhsT=codes_of[i][:, slot].bitcast(FP8X4),
                    lhsT_scale=scales_of[i][:, slot],
                    rhs=w_codes[name, c][:, part].bitcast(FP8X4),
                    rhs_scale=w_scales[name, c][:, part],
                    start=(name == "own"),
                    stop=(name == "others"),
                )
            cols = slice(c * N_PASS + first, c * N_PASS + first + N_LAST)
            copy(out=result_of[i][:, p, cols], in_=acc[:])
            store(i, p, cols)
